import numpy as np
import ml_dtypes


def mxq(x, axis, fmt="e4m3"):
    dtype, down = {"e4m3": (ml_dtypes.float8_e4m3fn, 7), "e5m2": (ml_dtypes.float8_e5m2, 14)}[fmt]
    v = np.moveaxis(np.asarray(x, np.float32).astype(ml_dtypes.bfloat16).astype(np.float64), axis, -1)
    blocks = v.reshape(v.shape[:-1] + (-1, 32))
    amax = np.abs(blocks).max(-1, keepdims=True)
    byte = np.maximum(np.where(amax > 0, np.frexp(amax)[1] - 1 + 127, 0) - down, 1)
    scale = np.exp2(byte - 127.0)
    codes = (blocks / scale).astype(np.float32).astype(dtype).astype(np.float64)
    return np.moveaxis((codes * scale).reshape(v.shape), -1, axis)


WIDE = False


def mx_kscale(k):
    if not WIDE:
        return np.ones(k)
    levels = np.array([10, -10, 5, -5, 0])
    if k % 512:
        return np.exp2(np.random.permutation(np.resize(levels, k // 32))).repeat(32)
    a = np.empty((k // 512, 16))
    for p in range(k // 512):
        a[p, :8] = np.random.permutation(np.resize(levels, 8))
        for g in range(8):
            far = levels[np.abs(levels - a[p, g]) >= 10]
            a[p, g + 8] = far[np.random.randint(len(far))]
    return np.exp2(a.ravel()).repeat(32)


BF16 = ml_dtypes.bfloat16


def bf(x):
    return np.asarray(x, np.float32).astype(BF16)


def f64(x):
    return np.asarray(x).astype(np.float64)


B, T, C, H, D, R = 4, 1024, 1024, 4, 128, 512
EPS = 1e-6
THETA = 10000.0


def rmsnorm(v, w):
    var = np.mean(v * v, axis=-1, keepdims=True)
    return v * (1.0 / np.sqrt(var + EPS)) * w


def rope(v, cos, sin):
    re, im = v[..., 0::2], v[..., 1::2]
    c, s = cos[None, :, None, :], sin[None, :, None, :]
    return np.stack([re * c - im * s, re * s + im * c], axis=-1).reshape(v.shape)


def draw0():
    s, t = mx_kscale(C), mx_kscale(R)
    ang = np.outer(np.arange(T), 1.0 / THETA ** (np.arange(0, D, 2) / D))
    return {"x": bf(np.random.standard_normal((B, T, C)) * s),
            "w_kv_down": bf(np.random.standard_normal((R, C)) / np.sqrt(C) / s[None, :] * t[:, None]),
            "w_kv_up": bf(np.random.standard_normal((2 * H * D, R)) / np.sqrt(R) / t[None, :]),
            "k_norm_w": bf(1.0 + 0.1 * np.random.standard_normal(D)),
            "freqs_cos": bf(np.cos(ang)), "freqs_sin": bf(np.sin(ang))}


def core(x, w_kv_down, w_kv_up, k_norm_w, freqs_cos, freqs_sin):
    latent = mxq(f64(x), 2, "e4m3") @ mxq(f64(w_kv_down), 1, "e4m3").T
    kv = (mxq(latent, 2, "e4m3") @ mxq(f64(w_kv_up), 1, "e4m3").T).reshape(B, T, 2, H, D)
    xk, xv = kv[:, :, 0], kv[:, :, 1]
    return rope(rmsnorm(xk, f64(k_norm_w)), f64(freqs_cos), f64(freqs_sin)), xv


def e4m3fn_bytes(y):
    return np.clip(np.asarray(y, np.float64), -448.0, 448.0).astype(np.float32).astype(ml_dtypes.float8_e4m3fn).view(np.uint8)


def e4m3fn_values(b):
    return np.asarray(b, np.uint8).view(ml_dtypes.float8_e4m3fn).astype(np.float64)


def setup_inputs():
    d = draw0()
    x0 = np.asarray(d['x']).astype(np.float64)
    s = (np.max(np.abs(x0), axis=(0, 1), keepdims=True) / 448.0).astype(np.float32)
    out = {}
    for k, v in d.items():
        if k == 'x':
            out['x_bytes'] = e4m3fn_bytes(x0 / s.astype(np.float64))
            out['x_scale'] = s
        else:
            out[k] = v
    return out


def reference(x_bytes, x_scale, w_kv_down, w_kv_up, k_norm_w, freqs_cos, freqs_sin):
    return core(e4m3fn_values(x_bytes) * x_scale.astype(np.float64), w_kv_down, w_kv_up, k_norm_w, freqs_cos, freqs_sin)

@@ -1,0 +1,338 @@
+from contextlib import ExitStack
+
+import concourse.mybir as mybir
+from concourse.masks import make_identity
+
+B, T, C, H, D, R = 4, 1024, 1024, 4, 128, 512
+EPS = 1e-6
+P = 128
+SUB = 128
+PAIRS = B * T // (2 * SUB)
+FEAT = H * D
+FLOPS = 2 * B * T * C * R + 2 * B * T * R * 2 * FEAT + 10 * B * T * FEAT
+
+F32 = mybir.dt.float32
+BF16 = mybir.dt.bfloat16
+U32 = mybir.dt.uint32
+U8 = mybir.dt.uint8
+FP8 = mybir.dt.float8_e4m3fn
+FP8X4 = mybir.dt.float8_e4m3fn_x4
+ACT = mybir.ActivationFunctionType
+ALU = mybir.AluOpType
+
+M_AHEAD = 2
+W_AHEAD = 4
+
+
+def tile_mla_pa_t_kernel(tc, x_bytes, x_scale, w_kv_down, w_kv_up, k_norm_w, freqs_cos, freqs_sin, out_0, out_1):
+    nc = tc.nc
+    with ExitStack() as ctx:
+        keep = ctx.enter_context(tc.tile_pool(name="keep", bufs=1))
+        work = ctx.enter_context(tc.tile_pool(name="work", bufs=3))
+        psum = ctx.enter_context(tc.psum_pool(name="psum", bufs=2))
+        ctx.enter_context(tc.manual_schedule())
+
+        eps_in = keep.tile([P, 1], F32)
+        nc.vector.memset(eps_in[:], 1.0)
+        eps_out = keep.tile([P, 1], F32)
+        nc.scalar.activation(out=eps_out[:], in_=eps_in[:], func=ACT.Abs_reciprocal_sqrt, bias=EPS, scale=1.0 / D)
+
+        scale = keep.tile([P, 2, 4], F32)
+        nc.gpsimd.dma_start(out=scale[:], in_=x_scale[0, 0].rearrange("(g p t) -> p g t", p=P, t=4))
+        ident = keep.tile([P, P], F32)
+        make_identity(nc, ident[:])
+
+        cos_sb = keep.tile([P, 2, 4, D // 2], BF16)
+        sin_sb = keep.tile([P, 2, 4, D // 2], BF16)
+        gain = keep.tile([P, D], BF16)
+        nc.gpsimd.dma_start(out=cos_sb[:], in_=freqs_cos.rearrange("(s p q) j -> p s q j", p=P, q=4))
+        nc.gpsimd.dma_start(out=sin_sb[:], in_=freqs_sin.rearrange("(s p q) j -> p s q j", p=P, q=4))
+        nc.gpsimd.dma_start(out=gain[:], in_=k_norm_w.partition_broadcast(P))
+
+        wd_raw = keep.tile([P, 4, C], BF16, align_bytes=64)
+        wu_raw = keep.tile([P, 8, R], BF16, align_bytes=64)
+        wd_view = w_kv_down.rearrange("(m t) k -> m t k", t=4)
+        wu_view = w_kv_up.rearrange("(c m) r -> m c r", m=P)
+        x_views = [x_bytes[b].rearrange("(s p q) k -> s p q k", p=P, q=4) for b in range(B)]
+
+        x_tiles = {}
+
+        def load_x(pair):
+            b, s, h = pair // 4, pair // 2 % 2, pair % 2
+            x_codes = work.tile([P, 2, C], U8, tag="x_codes", bufs=PAIRS, align_bytes=64, name="x_codes")
+            nc.sync.dma_start(out=x_codes[:], in_=x_views[b][s][:, 2 * h : 2 * h + 2, :])
+            x_tiles[pair] = x_codes
+
+        load_x(0)
+        nc.sync.dma_start(out=wd_raw[:, 0:2, :], in_=wd_view[:, 0:2, :])
+        load_x(1)
+        nc.sync.dma_start(out=wd_raw[:, 2:4, :], in_=wd_view[:, 2:4, :])
+        nc.sync.dma_start(out=wu_raw[:, 0:4, :], in_=wu_view[:, 0:4, :])
+        load_x(2)
+        nc.sync.dma_start(out=wu_raw[:, 4:8, :], in_=wu_view[:, 4:8, :])
+        for pair in range(3, PAIRS):
+            load_x(pair)
+
+        wn = keep.tile([P, D // 2, 2], F32)
+        gain_pairs = gain[:].rearrange("p (j e) -> p j e", e=2)
+        nc.gpsimd.tensor_scalar(out=wn[:, :, 0], in0=gain_pairs[:, :, 1], scalar1=-1.0, scalar2=None, op0=ALU.mult)
+        nc.gpsimd.tensor_copy(out=wn[:, :, 1], in_=gain_pairs[:, :, 0])
+        table_a = keep.tile([P, 8, D // 2, 2], F32)
+        table_b = keep.tile([P, 8, D // 2, 2], F32)
+        shape = [P, 8, D // 2, 2]
+        nc.gpsimd.tensor_tensor(
+            out=table_a[:],
+            in0=cos_sb[:].rearrange("p s q j -> p (s q) j").unsqueeze(3).broadcast_to(shape),
+            in1=gain_pairs.unsqueeze(1).broadcast_to(shape),
+            op=ALU.mult,
+        )
+        nc.gpsimd.tensor_tensor(
+            out=table_b[:],
+            in0=sin_sb[:].rearrange("p s q j -> p (s q) j").unsqueeze(3).broadcast_to(shape),
+            in1=wn[:].unsqueeze(1).broadcast_to(shape),
+            op=ALU.mult,
+        )
+
+        wd_grouped = keep.tile([P, 2, 2, 256, 4], BF16, align_bytes=64)
+        wu_grouped = keep.tile([P, 2, 512, 4], BF16, align_bytes=64)
+        wd_codes = keep.tile([P, 2, 2, 256], U32, align_bytes=64)
+        wd_scales = keep.tile([P, 2, 2, 256], U8, align_bytes=64)
+        wu_codes = keep.tile([P, 2, 512], U32, align_bytes=64)
+        wu_scales = keep.tile([P, 2, 512], U8, align_bytes=64)
+
+        banks = {}
+
+        def turn_words(bank, words, first, col0):
+            for u in range(2):
+                nc.tensor.transpose(bank[:, u, col0 : col0 + SUB], words[:, first + u : first + 256 : 2], ident[:])
+
+        def wd_turn(th, tag):
+            for g in range(2):
+                bank = psum.tile([P, 2, 256], F32, tag=tag, name=tag)
+                for i in range(2):
+                    turn_words(bank, wd_raw[:, 2 * th + i, :].bitcast(F32), 256 * g, SUB * i)
+                banks["wd", th, g] = bank
+
+        def wu_turn(half, tag):
+            for i in range(2):
+                bank = psum.tile([P, 2, 256], F32, tag=tag, name=tag)
+                for j in range(2):
+                    turn_words(bank, wu_raw[:, 4 * half + 2 * i + j, :].bitcast(F32), 0, SUB * j)
+                banks["wu", half, i] = bank
+
+        def copy_words(copy, grouped, bank):
+            copy(out=grouped.rearrange("p n t -> p (n t)").bitcast(F32).rearrange("p (n u) -> p n u", u=2), in_=bank[:].rearrange("p u n -> p n u"))
+
+        def wd_out(copy, th, g):
+            copy_words(copy, wd_grouped[:, th, g], banks["wd", th, g])
+
+        def wu_out(copy, half, i):
+            copy_words(copy, wu_grouped[:, half, 256 * i : 256 * (i + 1)], banks["wu", half, i])
+
+        def wd_quant(th):
+            nc.vector.quantize_mx(
+                out=wd_codes[:, th].rearrange("p g n -> p (g n)").bitcast(FP8X4),
+                scales=wd_scales[:, th].rearrange("p g n -> p (g n)"),
+                in_=wd_grouped[:, th].rearrange("p g n t -> p (g n t)"),
+            )
+
+        def wu_quant(half):
+            nc.vector.quantize_mx(out=wu_codes[:, half].bitcast(FP8X4), scales=wu_scales[:, half], in_=wu_grouped[:, half].rearrange("p n t -> p (n t)"))
+
+        wide, xt, xg, xq, xs = {}, {}, {}, {}, {}
+        lat, lq, ls, kb, vb = {}, {}, {}, {}, {}
+        rs, kout, vout = {}, {}, {}
+
+        def live(pair):
+            return 0 <= pair < PAIRS
+
+        def widen(pair):
+            if not live(pair):
+                return
+            x_wide = work.tile([P, 2, C], BF16, tag="x_wide", align_bytes=64, name="x_wide")
+            for a in range(2):
+                nc.scalar.copy(out=x_wide[:, a, :], in_=x_tiles[pair][:, a, :].bitcast(FP8))
+            wide[pair] = x_wide
+
+        def turn(pair, g):
+            if not live(pair):
+                return
+            bank = psum.tile([P, 2, 256], F32, tag="xt%d" % g, bufs=1, name="xt")
+            for a in range(2):
+                turn_words(bank, wide[pair][:, a, :].bitcast(F32), 256 * g, SUB * a)
+            xt[pair, g] = bank
+
+        def mult(pair, g):
+            if not live(pair):
+                return
+            if g == 0:
+                x_grouped = work.tile([P, 2, 256, 4], BF16, tag="x_grouped", align_bytes=64, name="x_grouped")
+                xg[pair] = x_grouped
+            nc.vector.tensor_tensor(
+                out=xg[pair][:, g].rearrange("p n (u e) -> p n u e", u=2),
+                in0=xt[pair, g][:].rearrange("p u n -> p (u n)").bitcast(BF16).rearrange("p (u n e) -> p n u e", u=2, e=2),
+                in1=scale[:, g, :].rearrange("p (u e) -> p u e", u=2).unsqueeze(1).broadcast_to([P, 256, 2, 2]),
+                op=ALU.mult,
+            )
+
+        def quant(pair):
+            if not live(pair):
+                return
+            x_q = work.tile([P, 2, 256], U32, tag="x_q", align_bytes=64, name="x_q")
+            x_s = work.tile([P, 2, 256], U8, tag="x_s", align_bytes=64, name="x_s")
+            nc.vector.quantize_mx(
+                out=x_q[:].rearrange("p g n -> p (g n)").bitcast(FP8X4),
+                scales=x_s[:].rearrange("p g n -> p (g n)"),
+                in_=xg[pair][:].rearrange("p g n t -> p (g n t)"),
+            )
+            xq[pair], xs[pair] = x_q, x_s
+
+        def down(pair, a):
+            if not live(pair):
+                return
+            bank = psum.tile([P, 4, SUB], F32, tag="lat", name="lat_ps")
+            cols = slice(SUB * a, SUB * (a + 1))
+            for t in range(4):
+                th, wcols = t // 2, slice(SUB * (t % 2), SUB * (t % 2 + 1))
+                for g in range(2):
+                    nc.tensor.matmul_mx(
+                        out=bank[:, t, :],
+                        lhsT=wd_codes[:, th, g, wcols].bitcast(FP8X4),
+                        lhsT_scale=wd_scales[:, th, g, wcols],
+                        rhs=xq[pair][:, g, cols].bitcast(FP8X4),
+                        rhs_scale=xs[pair][:, g, cols],
+                        start=(g == 0),
+                        stop=(g == 1),
+                    )
+            banks["lat", pair, a] = bank
+
+        def latent_out(pair, a):
+            if not live(pair):
+                return
+            if a == 0:
+                latent = work.tile([P, 2, SUB, 4], BF16, tag="latent", align_bytes=64, name="latent")
+                lat[pair] = latent
+            nc.scalar.copy(out=lat[pair][:, a], in_=banks["lat", pair, a][:].rearrange("p t n -> p n t"))
+
+        def latent_quant(pair):
+            if not live(pair):
+                return
+            l_q = work.tile([P, 2, SUB], U32, tag="l_q", align_bytes=64, name="l_q")
+            l_s = work.tile([P, 2, SUB], U8, tag="l_s", align_bytes=64, name="l_s")
+            nc.vector.quantize_mx(
+                out=l_q[:].rearrange("p a n -> p (a n)").bitcast(FP8X4),
+                scales=l_s[:].rearrange("p a n -> p (a n)"),
+                in_=lat[pair][:].rearrange("p a n t -> p (a n t)"),
+            )
+            lq[pair], ls[pair] = l_q, l_s
+
+        def up(pair, a):
+            if not live(pair):
+                return
+            for half, dest, tag in ((0, kb, "kb"), (1, vb, "vb")):
+                bank = psum.tile([P, FEAT], F32, tag=tag, name=tag)
+                nc.tensor.matmul_mx(
+                    out=bank[:],
+                    lhsT=lq[pair][:, a, :].bitcast(FP8X4),
+                    lhsT_scale=ls[pair][:, a, :],
+                    rhs=wu_codes[:, half].bitcast(FP8X4),
+                    rhs_scale=wu_scales[:, half],
+                    start=True,
+                    stop=True,
+                )
+                dest[pair, a] = bank
+
+        def norm(pair, a):
+            if not live(pair):
+                return
+            squares = work.tile([P, H], F32, tag="squares", bufs=4, name="squares")
+            rstd = work.tile([P, H], F32, tag="rstd", bufs=4, name="rstd")
+            for h in range(H):
+                junk = work.tile([P, D], BF16, tag="junk", bufs=4, name="junk")
+                nc.scalar.activation(out=junk[:], in_=kb[pair, a][:, D * h : D * (h + 1)], func=ACT.Square, accum_out=squares[:, h : h + 1])
+            nc.scalar.activation(out=rstd[:], in_=squares[:], func=ACT.Abs_reciprocal_sqrt, bias=EPS, scale=1.0 / D)
+            rs[pair, a] = rstd
+
+        def values_out(pair, a):
+            if not live(pair):
+                return
+            if a == 0:
+                v_tile = work.tile([P, 2, FEAT], F32, tag="v_tile", bufs=4, name="v_tile")
+                vout[pair] = v_tile
+            nc.scalar.copy(out=vout[pair][:, a, :], in_=vb[pair, a][:])
+            store(out_1, vout[pair], pair, a)
+
+        def store(out, tile, pair, a):
+            b, s, h = pair // 4, pair // 2 % 2, pair % 2
+            view = out[b].rearrange("(s p q) h d -> s p q (h d)", p=P, q=4)[s]
+            if pair == PAIRS - 1:
+                nc.sync.dma_start(out=view[:, 2 * h + a, :], in_=tile[:, a, :])
+            elif a == 1:
+                nc.sync.dma_start(out=view[:, 2 * h : 2 * h + 2, :], in_=tile[:])
+
+        def rotate(pair, a):
+            if not live(pair):
+                return
+            row = (pair // 2 % 2) * 4 + 2 * (pair % 2) + a
+            t1 = work.tile([P, FEAT], F32, tag="t1", name="t1")
+            t2 = work.tile([P, FEAT], F32, tag="t2", name="t2")
+            for h in range(H):
+                cols = slice(D * h, D * (h + 1))
+                nc.vector.scalar_tensor_tensor(
+                    out=t1[:, cols], in0=kb[pair, a][:, cols], scalar=rs[pair, a][:, h : h + 1],
+                    in1=table_a[:, row].rearrange("p j e -> p (j e)"), op0=ALU.mult, op1=ALU.mult,
+                )
+                nc.vector.scalar_tensor_tensor(
+                    out=t2[:, cols].rearrange("p (j e) -> p j e", e=2),
+                    in0=kb[pair, a][:, cols].rearrange("p (j e) -> p j e", e=2)[:, :, ::-1],
+                    scalar=rs[pair, a][:, h : h + 1],
+                    in1=table_b[:, row], op0=ALU.mult, op1=ALU.mult,
+                )
+            if a == 0:
+                k_tile = work.tile([P, 2, FEAT], F32, tag="k_tile", bufs=4, name="k_tile")
+                kout[pair] = k_tile
+            nc.gpsimd.tensor_tensor(out=kout[pair][:, a, :], in0=t1[:], in1=t2[:], op=ALU.add)
+            store(out_0, kout[pair], pair, a)
+
+        for s in range(-W_AHEAD, PAIRS + 1):
+            down(s, 0)
+            down(s, 1)
+            latent_out(s, 0)
+            latent_out(s, 1)
+            widen(s + W_AHEAD)
+            rotate(s - 1, 0)
+            turn(s + M_AHEAD, 1)
+            mult(s + M_AHEAD, 0)
+            turn(s + M_AHEAD + 1, 0)
+            if s == -2:
+                wd_turn(0, "lat")
+                wd_turn(1, "kb")
+                wd_out(nc.scalar.copy, 0, 0)
+                wd_out(nc.scalar.copy, 0, 1)
+            if s == -1:
+                wd_quant(0)
+                wu_turn(0, "vb")
+                wu_turn(1, "kb")
+                wu_out(nc.scalar.copy, 0, 0)
+                wu_out(nc.scalar.copy, 0, 1)
+            if s == 0:
+                wu_quant(1)
+            latent_quant(s)
+            rotate(s - 1, 1)
+            mult(s + M_AHEAD, 1)
+            if s == -2:
+                wd_out(nc.vector.tensor_copy, 1, 0)
+                wd_out(nc.vector.tensor_copy, 1, 1)
+            if s == -1:
+                wd_quant(1)
+            quant(s + M_AHEAD - 1)
+            if s == -1:
+                wu_out(nc.vector.tensor_copy, 1, 0)
+                wu_out(nc.vector.tensor_copy, 1, 1)
+                wu_quant(0)
+            up(s, 0)
+            norm(s, 0)
+            values_out(s, 0)
+            up(s, 1)
+            norm(s, 1)
+            values_out(s, 1)

@@ -20,8 +20,10 @@ FP8X4 = mybir.dt.float8_e4m3fn_x4
 ACT = mybir.ActivationFunctionType
 ALU = mybir.AluOpType
 
-M_AHEAD = 2
-W_AHEAD = 4
+TURN_AHEAD = 2
+MULT_AHEAD = 3
+BUFS = {"lat": 2, "kb": 3, "vb": 1}
+LATE = 3
 
 
 def tile_mla_pa_t_kernel(tc, x_bytes, x_scale, w_kv_down, w_kv_up, k_norm_w, freqs_cos, freqs_sin, out_0, out_1):
@@ -70,7 +72,10 @@ def tile_mla_pa_t_kernel(tc, x_bytes, x_scale, w_kv_down, w_kv_up, k_norm_w, fre
         nc.sync.dma_start(out=wu_raw[:, 0:4, :], in_=wu_view[:, 0:4, :])
         load_x(2)
         nc.sync.dma_start(out=wu_raw[:, 4:8, :], in_=wu_view[:, 4:8, :])
-        for pair in range(3, PAIRS):
+        load_x(3)
+        scale_row = keep.tile([P, C], F32)
+        nc.sync.dma_start(out=scale_row[:], in_=x_scale[0, 0].partition_broadcast(P))
+        for pair in range(4, PAIRS):
             load_x(pair)
 
         wn = keep.tile([P, D // 2, 2], F32)
@@ -108,14 +113,14 @@ def tile_mla_pa_t_kernel(tc, x_bytes, x_scale, w_kv_down, w_kv_up, k_norm_w, fre
 
         def wd_turn(th, tag):
             for g in range(2):
-                bank = psum.tile([P, 2, 256], F32, tag=tag, name=tag)
+                bank = psum.tile([P, 2, 256], F32, tag=tag, bufs=BUFS[tag], name="wd_ps")
                 for i in range(2):
                     turn_words(bank, wd_raw[:, 2 * th + i, :].bitcast(F32), 256 * g, SUB * i)
                 banks["wd", th, g] = bank
 
-        def wu_turn(half, tag):
+        def wu_turn(half, tags):
             for i in range(2):
-                bank = psum.tile([P, 2, 256], F32, tag=tag, name=tag)
+                bank = psum.tile([P, 2, 256], F32, tag=tags[i], bufs=BUFS[tags[i]], name="wu_ps")
                 for j in range(2):
                     turn_words(bank, wu_raw[:, 4 * half + 2 * i + j, :].bitcast(F32), 0, SUB * j)
                 banks["wu", half, i] = bank
@@ -141,18 +146,28 @@ def tile_mla_pa_t_kernel(tc, x_bytes, x_scale, w_kv_down, w_kv_up, k_norm_w, fre
 
         wide, xt, xg, xq, xs = {}, {}, {}, {}, {}
         lat, lq, ls, kb, vb = {}, {}, {}, {}, {}
-        rs, kout, vout = {}, {}, {}
+        rs, kout, vout, products = {}, {}, {}, {}
 
         def live(pair):
             return 0 <= pair < PAIRS
 
-        def widen(pair):
-            if not live(pair):
-                return
+        def wide_tile(pair):
             x_wide = work.tile([P, 2, C], BF16, tag="x_wide", align_bytes=64, name="x_wide")
-            for a in range(2):
-                nc.scalar.copy(out=x_wide[:, a, :], in_=x_tiles[pair][:, a, :].bitcast(FP8))
             wide[pair] = x_wide
+
+        def widen(pair, a, copy):
+            if not 0 <= pair < LATE:
+                return
+            if a == 0:
+                wide_tile(pair)
+            copy(out=wide[pair][:, a, :], in_=x_tiles[pair][:, a, :].bitcast(FP8))
+
+        def premult(pair, a):
+            if not LATE <= pair < PAIRS:
+                return
+            if a == 0:
+                wide_tile(pair)
+            nc.vector.tensor_tensor(out=wide[pair][:, a, :], in0=x_tiles[pair][:, a, :].bitcast(FP8), in1=scale_row[:], op=ALU.mult)
 
         def turn(pair, g):
             if not live(pair):
@@ -162,18 +177,21 @@ def tile_mla_pa_t_kernel(tc, x_bytes, x_scale, w_kv_down, w_kv_up, k_norm_w, fre
                 turn_words(bank, wide[pair][:, a, :].bitcast(F32), 256 * g, SUB * a)
             xt[pair, g] = bank
 
-        def mult(pair, g):
+        def x_out(pair, g):
             if not live(pair):
                 return
             if g == 0:
                 x_grouped = work.tile([P, 2, 256, 4], BF16, tag="x_grouped", align_bytes=64, name="x_grouped")
                 xg[pair] = x_grouped
-            nc.vector.tensor_tensor(
-                out=xg[pair][:, g].rearrange("p n (u e) -> p n u e", u=2),
-                in0=xt[pair, g][:].rearrange("p u n -> p (u n)").bitcast(BF16).rearrange("p (u n e) -> p n u e", u=2, e=2),
-                in1=scale[:, g, :].rearrange("p (u e) -> p u e", u=2).unsqueeze(1).broadcast_to([P, 256, 2, 2]),
-                op=ALU.mult,
-            )
+            if pair >= LATE:
+                copy_words(nc.scalar.copy, xg[pair][:, g], xt[pair, g])
+            else:
+                nc.vector.tensor_tensor(
+                    out=xg[pair][:, g].rearrange("p n (u e) -> p n u e", u=2),
+                    in0=xt[pair, g][:].rearrange("p u n -> p (u n)").bitcast(BF16).rearrange("p (u n e) -> p n u e", u=2, e=2),
+                    in1=scale[:, g, :].rearrange("p (u e) -> p u e", u=2).unsqueeze(1).broadcast_to([P, 256, 2, 2]),
+                    op=ALU.mult,
+                )
 
         def quant(pair):
             if not live(pair):
@@ -230,7 +248,7 @@ def tile_mla_pa_t_kernel(tc, x_bytes, x_scale, w_kv_down, w_kv_up, k_norm_w, fre
             if not live(pair):
                 return
             for half, dest, tag in ((0, kb, "kb"), (1, vb, "vb")):
-                bank = psum.tile([P, FEAT], F32, tag=tag, name=tag)
+                bank = psum.tile([P, FEAT], F32, tag=tag, bufs=BUFS[tag], name="kv_ps")
                 nc.tensor.matmul_mx(
                     out=bank[:],
                     lhsT=lq[pair][:, a, :].bitcast(FP8X4),
@@ -270,69 +288,96 @@ def tile_mla_pa_t_kernel(tc, x_bytes, x_scale, w_kv_down, w_kv_up, k_norm_w, fre
             elif a == 1:
                 nc.sync.dma_start(out=view[:, 2 * h : 2 * h + 2, :], in_=tile[:])
 
-        def rotate(pair, a):
+        def rotate(pair, a, first, last):
             if not live(pair):
                 return
             row = (pair // 2 % 2) * 4 + 2 * (pair % 2) + a
-            t1 = work.tile([P, FEAT], F32, tag="t1", name="t1")
-            t2 = work.tile([P, FEAT], F32, tag="t2", name="t2")
-            for h in range(H):
+            if first == 0:
+                t1 = work.tile([P, FEAT], F32, tag="t1", name="t1")
+                t2 = work.tile([P, FEAT], F32, tag="t2", name="t2")
+                products[pair, a] = t1, t2
+            t1, t2 = products[pair, a]
+            for i in range(first, last):
+                h = i // 2
                 cols = slice(D * h, D * (h + 1))
-                nc.vector.scalar_tensor_tensor(
-                    out=t1[:, cols], in0=kb[pair, a][:, cols], scalar=rs[pair, a][:, h : h + 1],
-                    in1=table_a[:, row].rearrange("p j e -> p (j e)"), op0=ALU.mult, op1=ALU.mult,
-                )
-                nc.vector.scalar_tensor_tensor(
-                    out=t2[:, cols].rearrange("p (j e) -> p j e", e=2),
-                    in0=kb[pair, a][:, cols].rearrange("p (j e) -> p j e", e=2)[:, :, ::-1],
-                    scalar=rs[pair, a][:, h : h + 1],
-                    in1=table_b[:, row], op0=ALU.mult, op1=ALU.mult,
-                )
+                if i % 2 == 0:
+                    nc.vector.scalar_tensor_tensor(
+                        out=t1[:, cols], in0=kb[pair, a][:, cols], scalar=rs[pair, a][:, h : h + 1],
+                        in1=table_a[:, row].rearrange("p j e -> p (j e)"), op0=ALU.mult, op1=ALU.mult,
+                    )
+                else:
+                    nc.vector.scalar_tensor_tensor(
+                        out=t2[:, cols].rearrange("p (j e) -> p j e", e=2),
+                        in0=kb[pair, a][:, cols].rearrange("p (j e) -> p j e", e=2)[:, :, ::-1],
+                        scalar=rs[pair, a][:, h : h + 1],
+                        in1=table_b[:, row], op0=ALU.mult, op1=ALU.mult,
+                    )
+
+        def keys_out(pair, a, engine):
+            if not live(pair):
+                return
             if a == 0:
                 k_tile = work.tile([P, 2, FEAT], F32, tag="k_tile", bufs=4, name="k_tile")
                 kout[pair] = k_tile
-            nc.gpsimd.tensor_tensor(out=kout[pair][:, a, :], in0=t1[:], in1=t2[:], op=ALU.add)
+            t1, t2 = products[pair, a]
+            engine.tensor_tensor(out=kout[pair][:, a, :], in0=t1[:], in1=t2[:], op=ALU.add)
             store(out_0, kout[pair], pair, a)
 
-        for s in range(-W_AHEAD, PAIRS + 1):
+        widen(0, 0, nc.vector.tensor_copy)
+        widen(0, 1, nc.scalar.copy)
+        turn(0, 0)
+        turn(0, 1)
+        for a in range(2):
+            widen(1, a, nc.scalar.copy)
+        x_out(0, 0)
+        x_out(0, 1)
+        wd_turn(0, "lat")
+        wd_turn(1, "kb")
+        wd_out(nc.scalar.copy, 0, 0)
+        wd_out(nc.scalar.copy, 0, 1)
+        turn(1, 0)
+        turn(1, 1)
+        wd_out(nc.vector.tensor_copy, 1, 0)
+        wd_out(nc.vector.tensor_copy, 1, 1)
+        for a in range(2):
+            widen(2, a, nc.scalar.copy)
+        wd_quant(0)
+        quant(0)
+        wd_quant(1)
+        wu_turn(0, ("vb", "kb"))
+        wu_turn(1, ("kb", "kb"))
+        wu_out(nc.scalar.copy, 0, 0)
+        wu_out(nc.scalar.copy, 0, 1)
+        x_out(1, 0)
+        x_out(1, 1)
+        wu_out(nc.vector.tensor_copy, 1, 0)
+        wu_out(nc.vector.tensor_copy, 1, 1)
+
+        for s in range(PAIRS + 1):
             down(s, 0)
             down(s, 1)
+            turn(s + TURN_AHEAD, 0)
+            turn(s + TURN_AHEAD, 1)
             latent_out(s, 0)
             latent_out(s, 1)
-            widen(s + W_AHEAD)
-            rotate(s - 1, 0)
-            turn(s + M_AHEAD, 1)
-            mult(s + M_AHEAD, 0)
-            turn(s + M_AHEAD + 1, 0)
-            if s == -2:
-                wd_turn(0, "lat")
-                wd_turn(1, "kb")
-                wd_out(nc.scalar.copy, 0, 0)
-                wd_out(nc.scalar.copy, 0, 1)
-            if s == -1:
-                wd_quant(0)
-                wu_turn(0, "vb")
-                wu_turn(1, "kb")
-                wu_out(nc.scalar.copy, 0, 0)
-                wu_out(nc.scalar.copy, 0, 1)
+            rotate(s - 2, 1, 7, 8)
+            keys_out(s - 2, 1, nc.gpsimd)
+            rotate(s - 1, 0, 0, 8)
+            keys_out(s - 1, 0, nc.gpsimd)
+            last = s == PAIRS
+            rotate(s - 1, 1, 0, 8 if last else 7)
+            if last:
+                keys_out(s - 1, 1, nc.vector)
+            x_out(s + TURN_AHEAD, 0)
+            x_out(s + TURN_AHEAD, 1)
             if s == 0:
+                wu_quant(0)
                 wu_quant(1)
             latent_quant(s)
-            rotate(s - 1, 1)
-            mult(s + M_AHEAD, 1)
-            if s == -2:
-                wd_out(nc.vector.tensor_copy, 1, 0)
-                wd_out(nc.vector.tensor_copy, 1, 1)
-            if s == -1:
-                wd_quant(1)
-            quant(s + M_AHEAD - 1)
-            if s == -1:
-                wu_out(nc.vector.tensor_copy, 1, 0)
-                wu_out(nc.vector.tensor_copy, 1, 1)
-                wu_quant(0)
-            up(s, 0)
-            norm(s, 0)
-            values_out(s, 0)
-            up(s, 1)
-            norm(s, 1)
-            values_out(s, 1)
+            premult(s + MULT_AHEAD, 0)
+            premult(s + MULT_AHEAD, 1)
+            quant(s + 1)
+            for a in range(2):
+                up(s, a)
+                norm(s, a)
+                values_out(s, a)

@@ -20,10 +20,10 @@ FP8X4 = mybir.dt.float8_e4m3fn_x4
 ACT = mybir.ActivationFunctionType
 ALU = mybir.AluOpType
 
-TURN_AHEAD = 2
-MULT_AHEAD = 3
-BUFS = {"lat": 2, "kb": 3, "vb": 1}
-LATE = 3
+BUFS = {"lat": 2, "kb": 2, "vb": 2, "xt0": 1, "xt1": 1}
+EARLY = 2
+AHEAD = 2
+WARM = 8
 
 
 def tile_mla_pa_t_kernel(tc, x_bytes, x_scale, w_kv_down, w_kv_up, k_norm_w, freqs_cos, freqs_sin, out_0, out_1):
@@ -39,24 +39,21 @@ def tile_mla_pa_t_kernel(tc, x_bytes, x_scale, w_kv_down, w_kv_up, k_norm_w, fre
         eps_out = keep.tile([P, 1], F32)
         nc.scalar.activation(out=eps_out[:], in_=eps_in[:], func=ACT.Abs_reciprocal_sqrt, bias=EPS, scale=1.0 / D)
 
-        scale = keep.tile([P, 2, 4], F32)
-        nc.gpsimd.dma_start(out=scale[:], in_=x_scale[0, 0].rearrange("(g p t) -> p g t", p=P, t=4))
+        warm = keep.tile([P, 512], BF16)
+        nc.vector.memset(warm[:], 0.0)
         ident = keep.tile([P, P], F32)
         make_identity(nc, ident[:])
 
+        scale = keep.tile([P, 2, 4], F32)
+        scale_row = keep.tile([P, C], F32)
         cos_sb = keep.tile([P, 2, 4, D // 2], BF16)
         sin_sb = keep.tile([P, 2, 4, D // 2], BF16)
         gain = keep.tile([P, D], BF16)
-        nc.gpsimd.dma_start(out=cos_sb[:], in_=freqs_cos.rearrange("(s p q) j -> p s q j", p=P, q=4))
-        nc.gpsimd.dma_start(out=sin_sb[:], in_=freqs_sin.rearrange("(s p q) j -> p s q j", p=P, q=4))
-        nc.gpsimd.dma_start(out=gain[:], in_=k_norm_w.partition_broadcast(P))
-
         wd_raw = keep.tile([P, 4, C], BF16, align_bytes=64)
         wu_raw = keep.tile([P, 8, R], BF16, align_bytes=64)
         wd_view = w_kv_down.rearrange("(m t) k -> m t k", t=4)
         wu_view = w_kv_up.rearrange("(c m) r -> m c r", m=P)
         x_views = [x_bytes[b].rearrange("(s p q) k -> s p q k", p=P, q=4) for b in range(B)]
-
         x_tiles = {}
 
         def load_x(pair):
@@ -65,36 +62,38 @@ def tile_mla_pa_t_kernel(tc, x_bytes, x_scale, w_kv_down, w_kv_up, k_norm_w, fre
             nc.sync.dma_start(out=x_codes[:], in_=x_views[b][s][:, 2 * h : 2 * h + 2, :])
             x_tiles[pair] = x_codes
 
+        nc.scalar.dma_start(out=gain[:], in_=k_norm_w.partition_broadcast(P))
         load_x(0)
+        nc.sync.dma_start(out=scale[:], in_=x_scale[0, 0].rearrange("(g p t) -> p g t", p=P, t=4))
         nc.sync.dma_start(out=wd_raw[:, 0:2, :], in_=wd_view[:, 0:2, :])
+        nc.sync.dma_start(out=cos_sb[:], in_=freqs_cos.rearrange("(s p q) j -> p s q j", p=P, q=4))
+        nc.sync.dma_start(out=sin_sb[:], in_=freqs_sin.rearrange("(s p q) j -> p s q j", p=P, q=4))
         load_x(1)
         nc.sync.dma_start(out=wd_raw[:, 2:4, :], in_=wd_view[:, 2:4, :])
-        nc.sync.dma_start(out=wu_raw[:, 0:4, :], in_=wu_view[:, 0:4, :])
-        load_x(2)
-        nc.sync.dma_start(out=wu_raw[:, 4:8, :], in_=wu_view[:, 4:8, :])
-        load_x(3)
-        scale_row = keep.tile([P, C], F32)
         nc.sync.dma_start(out=scale_row[:], in_=x_scale[0, 0].partition_broadcast(P))
-        for pair in range(4, PAIRS):
+        load_x(2)
+        nc.sync.dma_start(out=wu_raw[:, 0:4, :], in_=wu_view[:, 0:4, :])
+        nc.sync.dma_start(out=wu_raw[:, 4:8, :], in_=wu_view[:, 4:8, :])
+        for pair in range(3, PAIRS):
             load_x(pair)
 
-        wn = keep.tile([P, D // 2, 2], F32)
+        half = D // 2
         gain_pairs = gain[:].rearrange("p (j e) -> p j e", e=2)
-        nc.gpsimd.tensor_scalar(out=wn[:, :, 0], in0=gain_pairs[:, :, 1], scalar1=-1.0, scalar2=None, op0=ALU.mult)
-        nc.gpsimd.tensor_copy(out=wn[:, :, 1], in_=gain_pairs[:, :, 0])
-        table_a = keep.tile([P, 8, D // 2, 2], F32)
-        table_b = keep.tile([P, 8, D // 2, 2], F32)
-        shape = [P, 8, D // 2, 2]
+        gain_crossed = keep.tile([P, 2, half], F32)
+        nc.gpsimd.tensor_scalar(out=gain_crossed[:, 0], in0=gain_pairs[:, :, 1], scalar1=-1.0, scalar2=None, op0=ALU.mult)
+        nc.gpsimd.tensor_copy(out=gain_crossed[:, 1], in_=gain_pairs[:, :, 0])
+        table_a = keep.tile([P, 8, half, 2], F32)
+        table_b = keep.tile([P, 8, 2, half], F32)
         nc.gpsimd.tensor_tensor(
             out=table_a[:],
-            in0=cos_sb[:].rearrange("p s q j -> p (s q) j").unsqueeze(3).broadcast_to(shape),
-            in1=gain_pairs.unsqueeze(1).broadcast_to(shape),
+            in0=cos_sb[:].rearrange("p s q j -> p (s q) j").unsqueeze(3).broadcast_to([P, 8, half, 2]),
+            in1=gain_pairs.unsqueeze(1).broadcast_to([P, 8, half, 2]),
             op=ALU.mult,
         )
         nc.gpsimd.tensor_tensor(
             out=table_b[:],
-            in0=sin_sb[:].rearrange("p s q j -> p (s q) j").unsqueeze(3).broadcast_to(shape),
-            in1=wn[:].unsqueeze(1).broadcast_to(shape),
+            in0=sin_sb[:].rearrange("p s q j -> p (s q) j").unsqueeze(2).broadcast_to([P, 8, 2, half]),
+            in1=gain_crossed[:].unsqueeze(1).broadcast_to([P, 8, 2, half]),
             op=ALU.mult,
         )
 
@@ -107,23 +106,32 @@ def tile_mla_pa_t_kernel(tc, x_bytes, x_scale, w_kv_down, w_kv_up, k_norm_w, fre
 
         banks = {}
 
-        def turn_words(bank, words, first, col0):
+        def bank_tile(tag, shape):
+            bank = psum.tile(shape, F32, tag=tag, bufs=BUFS[tag], name="bank")
+            return bank
+
+        def warm_up(count):
+            for n in range(count):
+                bank = bank_tile("vb", [P, 512])
+                nc.tensor.matmul(bank[:], lhsT=warm[:, 0:P], rhs=warm[:], start=True, stop=True)
+
+        def turn_words(out, words, first):
             for u in range(2):
-                nc.tensor.transpose(bank[:, u, col0 : col0 + SUB], words[:, first + u : first + 256 : 2], ident[:])
+                nc.tensor.transpose(out[:, u], words[:, first + u : first + 256 : 2], ident[:])
 
         def wd_turn(th, tag):
             for g in range(2):
-                bank = psum.tile([P, 2, 256], F32, tag=tag, bufs=BUFS[tag], name="wd_ps")
+                bank = bank_tile(tag, [P, 2, 256])
                 for i in range(2):
-                    turn_words(bank, wd_raw[:, 2 * th + i, :].bitcast(F32), 256 * g, SUB * i)
+                    turn_words(bank[:, :, SUB * i : SUB * (i + 1)], wd_raw[:, 2 * th + i, :].bitcast(F32), 256 * g)
                 banks["wd", th, g] = bank
 
-        def wu_turn(half, tags):
+        def wu_turn(part, tags):
             for i in range(2):
-                bank = psum.tile([P, 2, 256], F32, tag=tags[i], bufs=BUFS[tags[i]], name="wu_ps")
+                bank = bank_tile(tags[i], [P, 2, 256])
                 for j in range(2):
-                    turn_words(bank, wu_raw[:, 4 * half + 2 * i + j, :].bitcast(F32), 0, SUB * j)
-                banks["wu", half, i] = bank
+                    turn_words(bank[:, :, SUB * j : SUB * (j + 1)], wu_raw[:, 4 * part + 2 * i + j, :].bitcast(F32), 0)
+                banks["wu", part, i] = bank
 
         def copy_words(copy, grouped, bank):
             copy(out=grouped.rearrange("p n t -> p (n t)").bitcast(F32).rearrange("p (n u) -> p n u", u=2), in_=bank[:].rearrange("p u n -> p n u"))
@@ -131,8 +139,8 @@ def tile_mla_pa_t_kernel(tc, x_bytes, x_scale, w_kv_down, w_kv_up, k_norm_w, fre
         def wd_out(copy, th, g):
             copy_words(copy, wd_grouped[:, th, g], banks["wd", th, g])
 
-        def wu_out(copy, half, i):
-            copy_words(copy, wu_grouped[:, half, 256 * i : 256 * (i + 1)], banks["wu", half, i])
+        def wu_out(copy, part, i):
+            copy_words(copy, wu_grouped[:, part, 256 * i : 256 * (i + 1)], banks["wu", part, i])
 
         def wd_quant(th):
             nc.vector.quantize_mx(
@@ -141,29 +149,26 @@ def tile_mla_pa_t_kernel(tc, x_bytes, x_scale, w_kv_down, w_kv_up, k_norm_w, fre
                 in_=wd_grouped[:, th].rearrange("p g n t -> p (g n t)"),
             )
 
-        def wu_quant(half):
-            nc.vector.quantize_mx(out=wu_codes[:, half].bitcast(FP8X4), scales=wu_scales[:, half], in_=wu_grouped[:, half].rearrange("p n t -> p (n t)"))
+        def wu_quant(part):
+            nc.vector.quantize_mx(out=wu_codes[:, part].bitcast(FP8X4), scales=wu_scales[:, part], in_=wu_grouped[:, part].rearrange("p n t -> p (n t)"))
 
-        wide, xt, xg, xq, xs = {}, {}, {}, {}, {}
-        lat, lq, ls, kb, vb = {}, {}, {}, {}, {}
-        rs, kout, vout, products = {}, {}, {}, {}
+        wide, xg, xq, xs, lat, lq, ls, rs, products = {}, {}, {}, {}, {}, {}, {}, {}, {}
+        kout, vout = {}, {}
 
         def live(pair):
             return 0 <= pair < PAIRS
 
         def wide_tile(pair):
-            x_wide = work.tile([P, 2, C], BF16, tag="x_wide", align_bytes=64, name="x_wide")
+            x_wide = work.tile([P, 2, C], BF16, tag="x_wide", bufs=AHEAD + 1, align_bytes=64, name="x_wide")
             wide[pair] = x_wide
 
         def widen(pair, a, copy):
-            if not 0 <= pair < LATE:
-                return
             if a == 0:
                 wide_tile(pair)
             copy(out=wide[pair][:, a, :], in_=x_tiles[pair][:, a, :].bitcast(FP8))
 
         def premult(pair, a):
-            if not LATE <= pair < PAIRS:
+            if not EARLY <= pair < PAIRS:
                 return
             if a == 0:
                 wide_tile(pair)
@@ -172,23 +177,24 @@ def tile_mla_pa_t_kernel(tc, x_bytes, x_scale, w_kv_down, w_kv_up, k_norm_w, fre
         def turn(pair, g):
             if not live(pair):
                 return
-            bank = psum.tile([P, 2, 256], F32, tag="xt%d" % g, bufs=1, name="xt")
+            bank = bank_tile("xt%d" % g, [P, 2, 256])
             for a in range(2):
-                turn_words(bank, wide[pair][:, a, :].bitcast(F32), 256 * g, SUB * a)
-            xt[pair, g] = bank
+                turn_words(bank[:, :, SUB * a : SUB * (a + 1)], wide[pair][:, a, :].bitcast(F32), 256 * g)
+            banks["xt", pair, g] = bank
 
-        def x_out(pair, g):
+        def x_out(pair, g, copy=nc.scalar.copy):
             if not live(pair):
                 return
             if g == 0:
                 x_grouped = work.tile([P, 2, 256, 4], BF16, tag="x_grouped", align_bytes=64, name="x_grouped")
                 xg[pair] = x_grouped
-            if pair >= LATE:
-                copy_words(nc.scalar.copy, xg[pair][:, g], xt[pair, g])
+            bank = banks["xt", pair, g]
+            if pair >= EARLY:
+                copy_words(copy, xg[pair][:, g], bank)
             else:
                 nc.vector.tensor_tensor(
                     out=xg[pair][:, g].rearrange("p n (u e) -> p n u e", u=2),
-                    in0=xt[pair, g][:].rearrange("p u n -> p (u n)").bitcast(BF16).rearrange("p (u n e) -> p n u e", u=2, e=2),
+                    in0=bank[:].rearrange("p u n -> p (u n)").bitcast(BF16).rearrange("p (u n e) -> p n u e", u=2, e=2),
                     in1=scale[:, g, :].rearrange("p (u e) -> p u e", u=2).unsqueeze(1).broadcast_to([P, 256, 2, 2]),
                     op=ALU.mult,
                 )
@@ -196,8 +202,8 @@ def tile_mla_pa_t_kernel(tc, x_bytes, x_scale, w_kv_down, w_kv_up, k_norm_w, fre
         def quant(pair):
             if not live(pair):
                 return
-            x_q = work.tile([P, 2, 256], U32, tag="x_q", align_bytes=64, name="x_q")
-            x_s = work.tile([P, 2, 256], U8, tag="x_s", align_bytes=64, name="x_s")
+            x_q = work.tile([P, 2, 256], U32, tag="x_q", bufs=AHEAD + 1, align_bytes=64, name="x_q")
+            x_s = work.tile([P, 2, 256], U8, tag="x_s", bufs=AHEAD + 1, align_bytes=64, name="x_s")
             nc.vector.quantize_mx(
                 out=x_q[:].rearrange("p g n -> p (g n)").bitcast(FP8X4),
                 scales=x_s[:].rearrange("p g n -> p (g n)"),
@@ -208,7 +214,7 @@ def tile_mla_pa_t_kernel(tc, x_bytes, x_scale, w_kv_down, w_kv_up, k_norm_w, fre
         def down(pair, a):
             if not live(pair):
                 return
-            bank = psum.tile([P, 4, SUB], F32, tag="lat", name="lat_ps")
+            bank = bank_tile("lat", [P, 4, SUB])
             cols = slice(SUB * a, SUB * (a + 1))
             for t in range(4):
                 th, wcols = t // 2, slice(SUB * (t % 2), SUB * (t % 2 + 1))
@@ -224,41 +230,57 @@ def tile_mla_pa_t_kernel(tc, x_bytes, x_scale, w_kv_down, w_kv_up, k_norm_w, fre
                     )
             banks["lat", pair, a] = bank
 
-        def latent_out(pair, a):
+        def latent_out(pair, a, copy=nc.scalar.copy):
             if not live(pair):
                 return
-            if a == 0:
-                latent = work.tile([P, 2, SUB, 4], BF16, tag="latent", align_bytes=64, name="latent")
-                lat[pair] = latent
-            nc.scalar.copy(out=lat[pair][:, a], in_=banks["lat", pair, a][:].rearrange("p t n -> p n t"))
+            latent = work.tile([P, SUB, 4], BF16, tag="latent", bufs=4, align_bytes=64, name="latent")
+            copy(out=latent[:], in_=banks["lat", pair, a][:].rearrange("p t n -> p n t"))
+            lat[pair, a] = latent
 
-        def latent_quant(pair):
+        def latent_quant(pair, a):
             if not live(pair):
                 return
-            l_q = work.tile([P, 2, SUB], U32, tag="l_q", align_bytes=64, name="l_q")
-            l_s = work.tile([P, 2, SUB], U8, tag="l_s", align_bytes=64, name="l_s")
-            nc.vector.quantize_mx(
-                out=l_q[:].rearrange("p a n -> p (a n)").bitcast(FP8X4),
-                scales=l_s[:].rearrange("p a n -> p (a n)"),
-                in_=lat[pair][:].rearrange("p a n t -> p (a n t)"),
+            l_q = work.tile([P, SUB], U32, tag="l_q", bufs=4, align_bytes=64, name="l_q")
+            l_s = work.tile([P, SUB], U8, tag="l_s", bufs=4, align_bytes=64, name="l_s")
+            nc.vector.quantize_mx(out=l_q[:].bitcast(FP8X4), scales=l_s[:], in_=lat[pair, a][:].rearrange("p n t -> p (n t)"))
+            lq[pair, a], ls[pair, a] = l_q, l_s
+
+        def up_pass(bank, pair, a, part):
+            nc.tensor.matmul_mx(
+                out=bank[:],
+                lhsT=lq[pair, a][:].bitcast(FP8X4),
+                lhsT_scale=ls[pair, a][:],
+                rhs=wu_codes[:, part].bitcast(FP8X4),
+                rhs_scale=wu_scales[:, part],
+                start=True,
+                stop=True,
             )
-            lq[pair], ls[pair] = l_q, l_s
 
-        def up(pair, a):
+        def up(pair):
             if not live(pair):
                 return
-            for half, dest, tag in ((0, kb, "kb"), (1, vb, "vb")):
-                bank = psum.tile([P, FEAT], F32, tag=tag, bufs=BUFS[tag], name="kv_ps")
+            for part, tag in ((0, "kb"), (1, "vb")):
+                for a in range(2):
+                    if (tag, pair, a) not in banks:
+                        bank = bank_tile(tag, [P, FEAT])
+                        banks[tag, pair, a] = bank
+                    up_pass(banks[tag, pair, a], pair, a, part)
+
+        def keep_warm(pair, count):
+            if not live(pair):
+                return
+            bank = bank_tile("kb", [P, FEAT])
+            for n in range(count):
                 nc.tensor.matmul_mx(
                     out=bank[:],
-                    lhsT=lq[pair][:, a, :].bitcast(FP8X4),
-                    lhsT_scale=ls[pair][:, a, :],
-                    rhs=wu_codes[:, half].bitcast(FP8X4),
-                    rhs_scale=wu_scales[:, half],
+                    lhsT=wd_codes[:, 0, 0, 0:P].bitcast(FP8X4),
+                    lhsT_scale=wd_scales[:, 0, 0, 0:P],
+                    rhs=wu_codes[:, 0].bitcast(FP8X4),
+                    rhs_scale=wu_scales[:, 0],
                     start=True,
                     stop=True,
                 )
-                dest[pair, a] = bank
+            banks["kb", pair, 0] = bank
 
         def norm(pair, a):
             if not live(pair):
@@ -267,18 +289,9 @@ def tile_mla_pa_t_kernel(tc, x_bytes, x_scale, w_kv_down, w_kv_up, k_norm_w, fre
             rstd = work.tile([P, H], F32, tag="rstd", bufs=4, name="rstd")
             for h in range(H):
                 junk = work.tile([P, D], BF16, tag="junk", bufs=4, name="junk")
-                nc.scalar.activation(out=junk[:], in_=kb[pair, a][:, D * h : D * (h + 1)], func=ACT.Square, accum_out=squares[:, h : h + 1])
+                nc.scalar.activation(out=junk[:], in_=banks["kb", pair, a][:, D * h : D * (h + 1)], func=ACT.Square, accum_out=squares[:, h : h + 1])
             nc.scalar.activation(out=rstd[:], in_=squares[:], func=ACT.Abs_reciprocal_sqrt, bias=EPS, scale=1.0 / D)
             rs[pair, a] = rstd
-
-        def values_out(pair, a):
-            if not live(pair):
-                return
-            if a == 0:
-                v_tile = work.tile([P, 2, FEAT], F32, tag="v_tile", bufs=4, name="v_tile")
-                vout[pair] = v_tile
-            nc.scalar.copy(out=vout[pair][:, a, :], in_=vb[pair, a][:])
-            store(out_1, vout[pair], pair, a)
 
         def store(out, tile, pair, a):
             b, s, h = pair // 4, pair // 2 % 2, pair % 2
@@ -288,96 +301,146 @@ def tile_mla_pa_t_kernel(tc, x_bytes, x_scale, w_kv_down, w_kv_up, k_norm_w, fre
             elif a == 1:
                 nc.sync.dma_start(out=view[:, 2 * h : 2 * h + 2, :], in_=tile[:])
 
+        def values_out(pair, a, copy):
+            if not live(pair):
+                return
+            if a == 0:
+                v_tile = work.tile([P, 2, FEAT], F32, tag="v_tile", bufs=4, name="v_tile")
+                vout[pair] = v_tile
+            copy(out=vout[pair][:, a, :], in_=banks["vb", pair, a][:])
+            store(out_1, vout[pair], pair, a)
+
+        def posted(pair, a):
+            return a == 0
+
         def rotate(pair, a, first, last):
             if not live(pair):
                 return
-            row = (pair // 2 % 2) * 4 + 2 * (pair % 2) + a
+            row = (2 * pair + a) % 8
             if first == 0:
-                t1 = work.tile([P, FEAT], F32, tag="t1", name="t1")
-                t2 = work.tile([P, FEAT], F32, tag="t2", name="t2")
+                t1 = work.tile([P, H, D], F32, tag="t1", name="t1")
+                t2 = work.tile([P, H, 2, half], F32, tag="t2", name="t2")
                 products[pair, a] = t1, t2
             t1, t2 = products[pair, a]
-            for i in range(first, last):
-                h = i // 2
-                cols = slice(D * h, D * (h + 1))
-                if i % 2 == 0:
-                    nc.vector.scalar_tensor_tensor(
-                        out=t1[:, cols], in0=kb[pair, a][:, cols], scalar=rs[pair, a][:, h : h + 1],
-                        in1=table_a[:, row].rearrange("p j e -> p (j e)"), op0=ALU.mult, op1=ALU.mult,
+            k = banks["kb", pair, a][:].rearrange("p (h d) -> p h d", h=H)
+            straight = table_a[:, row].rearrange("p j e -> p (j e)")
+            if posted(pair, a):
+                if first == 0:
+                    nc.vector.tensor_tensor(out=t1[:], in0=k, in1=straight.unsqueeze(1).broadcast_to([P, H, D]), op=ALU.mult)
+                if last == 8:
+                    nc.vector.tensor_tensor(
+                        out=t2[:].rearrange("p h e j -> p e h j"),
+                        in0=k.rearrange("p h (j e) -> p e h j", e=2)[:, ::-1],
+                        in1=table_b[:, row].unsqueeze(2).broadcast_to([P, 2, H, half]),
+                        op=ALU.mult,
                     )
+                return
+            for n in range(first, last):
+                h = n // 2
+                if n % 2 == 0:
+                    nc.vector.scalar_tensor_tensor(out=t1[:, h], in0=k[:, h], scalar=rs[pair, a][:, h : h + 1], in1=straight, op0=ALU.mult, op1=ALU.mult)
                 else:
                     nc.vector.scalar_tensor_tensor(
-                        out=t2[:, cols].rearrange("p (j e) -> p j e", e=2),
-                        in0=kb[pair, a][:, cols].rearrange("p (j e) -> p j e", e=2)[:, :, ::-1],
-                        scalar=rs[pair, a][:, h : h + 1],
+                        out=t2[:, h], in0=k[:, h].rearrange("p (j e) -> p e j", e=2)[:, ::-1], scalar=rs[pair, a][:, h : h + 1],
                         in1=table_b[:, row], op0=ALU.mult, op1=ALU.mult,
                     )
 
-        def keys_out(pair, a, engine):
+        def keys_out(pair, a, adder):
             if not live(pair):
                 return
             if a == 0:
                 k_tile = work.tile([P, 2, FEAT], F32, tag="k_tile", bufs=4, name="k_tile")
                 kout[pair] = k_tile
             t1, t2 = products[pair, a]
-            engine.tensor_tensor(out=kout[pair][:, a, :], in0=t1[:], in1=t2[:], op=ALU.add)
+            adder.tensor_tensor(
+                out=kout[pair][:, a, :].rearrange("p (h j e) -> p h j e", h=H, e=2),
+                in0=t1[:].rearrange("p h (j e) -> p h j e", e=2),
+                in1=t2[:].rearrange("p h e j -> p h j e"),
+                op=ALU.add,
+            )
+
+        def post(pair, a):
+            if not live(pair):
+                return
+            if not posted(pair, a):
+                store(out_0, kout[pair], pair, a)
+                return
+            for h in range(H):
+                head = kout[pair][:, a, D * h : D * (h + 1)]
+                nc.scalar.activation(out=head, in_=head, func=ACT.Copy, scale=rs[pair, a][:, h : h + 1])
             store(out_0, kout[pair], pair, a)
 
+        warm_up(WARM)
         widen(0, 0, nc.vector.tensor_copy)
         widen(0, 1, nc.scalar.copy)
         turn(0, 0)
         turn(0, 1)
-        for a in range(2):
-            widen(1, a, nc.scalar.copy)
+        warm_up(2)
+        widen(1, 0, nc.scalar.copy)
+        widen(1, 1, nc.scalar.copy)
         x_out(0, 0)
         x_out(0, 1)
         wd_turn(0, "lat")
+        warm_up(2)
         wd_turn(1, "kb")
-        wd_out(nc.scalar.copy, 0, 0)
-        wd_out(nc.scalar.copy, 0, 1)
+        warm_up(2)
         turn(1, 0)
         turn(1, 1)
-        wd_out(nc.vector.tensor_copy, 1, 0)
+        warm_up(1)
+        wd_out(nc.scalar.copy, 0, 0)
+        wd_out(nc.vector.tensor_copy, 0, 1)
+        wd_out(nc.scalar.copy, 1, 0)
         wd_out(nc.vector.tensor_copy, 1, 1)
-        for a in range(2):
-            widen(2, a, nc.scalar.copy)
-        wd_quant(0)
         quant(0)
+        wd_quant(0)
         wd_quant(1)
-        wu_turn(0, ("vb", "kb"))
-        wu_turn(1, ("kb", "kb"))
+        wu_turn(0, ("vb", "vb"))
+        down(0, 0)
+        down(0, 1)
         wu_out(nc.scalar.copy, 0, 0)
         wu_out(nc.scalar.copy, 0, 1)
+        premult(2, 0)
         x_out(1, 0)
+        wu_turn(1, ("kb", "kb"))
+        latent_out(0, 0)
+        latent_out(0, 1)
+        premult(2, 1)
         x_out(1, 1)
-        wu_out(nc.vector.tensor_copy, 1, 0)
-        wu_out(nc.vector.tensor_copy, 1, 1)
+        wu_quant(0)
+        latent_quant(0, 0)
+        latent_quant(0, 1)
+        wu_out(nc.scalar.copy, 1, 0)
+        wu_out(nc.scalar.copy, 1, 1)
+        quant(1)
+        wu_quant(1)
+        for pair in range(3, AHEAD + 1):
+            premult(pair, 0)
+            premult(pair, 1)
 
-        for s in range(PAIRS + 1):
+        for s in range(1, PAIRS + 1):
+            up(s - 1)
             down(s, 0)
             down(s, 1)
-            turn(s + TURN_AHEAD, 0)
-            turn(s + TURN_AHEAD, 1)
+            turn(s + 1, 0)
+            turn(s + 1, 1)
+            post(s - 2, 0)
+            post(s - 2, 1)
+            norm(s - 1, 0)
+            norm(s - 1, 1)
+            premult(s + AHEAD, 0)
+            premult(s + AHEAD, 1)
+            for a in range(2):
+                rotate(s - 1, a, 0, 8)
+                keys_out(s - 1, a, nc.vector if s == PAIRS and a == 1 else nc.gpsimd)
+            keep_warm(s, 2)
             latent_out(s, 0)
             latent_out(s, 1)
-            rotate(s - 2, 1, 7, 8)
-            keys_out(s - 2, 1, nc.gpsimd)
-            rotate(s - 1, 0, 0, 8)
-            keys_out(s - 1, 0, nc.gpsimd)
-            last = s == PAIRS
-            rotate(s - 1, 1, 0, 8 if last else 7)
-            if last:
-                keys_out(s - 1, 1, nc.vector)
-            x_out(s + TURN_AHEAD, 0)
-            x_out(s + TURN_AHEAD, 1)
-            if s == 0:
-                wu_quant(0)
-                wu_quant(1)
-            latent_quant(s)
-            premult(s + MULT_AHEAD, 0)
-            premult(s + MULT_AHEAD, 1)
+            x_out(s + 1, 0)
+            x_out(s + 1, 1)
+            values_out(s - 1, 0, nc.scalar.copy)
+            values_out(s - 1, 1, nc.scalar.copy)
+            latent_quant(s, 0)
+            latent_quant(s, 1)
             quant(s + 1)
-            for a in range(2):
-                up(s, a)
-                norm(s, a)
-                values_out(s, a)
+        post(PAIRS - 1, 0)
+        post(PAIRS - 1, 1)

from contextlib import ExitStack

import concourse.mybir as mybir
from concourse.masks import make_identity

B, T, C, H, D, R = 4, 1024, 1024, 4, 128, 512
EPS = 1e-6
P = 128
SUB = 128
PAIRS = B * T // (2 * SUB)
FEAT = H * D
FLOPS = 2 * B * T * C * R + 2 * B * T * R * 2 * FEAT + 10 * B * T * FEAT

F32 = mybir.dt.float32
BF16 = mybir.dt.bfloat16
U32 = mybir.dt.uint32
U8 = mybir.dt.uint8
FP8 = mybir.dt.float8_e4m3fn
FP8X4 = mybir.dt.float8_e4m3fn_x4
ACT = mybir.ActivationFunctionType
ALU = mybir.AluOpType

BUFS = {"lat": 2, "kb": 2, "vb": 2, "xt0": 1, "xt1": 1}
EARLY = 2
AHEAD = 2
WARM = 8


def tile_mla_pa_t_kernel(tc, x_bytes, x_scale, w_kv_down, w_kv_up, k_norm_w, freqs_cos, freqs_sin, out_0, out_1):
    nc = tc.nc
    with ExitStack() as ctx:
        keep = ctx.enter_context(tc.tile_pool(name="keep", bufs=1))
        work = ctx.enter_context(tc.tile_pool(name="work", bufs=3))
        psum = ctx.enter_context(tc.psum_pool(name="psum", bufs=2))
        ctx.enter_context(tc.manual_schedule())

        eps_in = keep.tile([P, 1], F32)
        nc.vector.memset(eps_in[:], 1.0)
        eps_out = keep.tile([P, 1], F32)
        nc.scalar.activation(out=eps_out[:], in_=eps_in[:], func=ACT.Abs_reciprocal_sqrt, bias=EPS, scale=1.0 / D)

        warm = keep.tile([P, 512], BF16)
        nc.vector.memset(warm[:], 0.0)
        ident = keep.tile([P, P], F32)
        make_identity(nc, ident[:])

        scale = keep.tile([P, 2, 4], F32)
        scale_row = keep.tile([P, C], F32)
        cos_sb = keep.tile([P, 2, 4, D // 2], BF16)
        sin_sb = keep.tile([P, 2, 4, D // 2], BF16)
        gain = keep.tile([P, D], BF16)
        wd_raw = keep.tile([P, 4, C], BF16, align_bytes=64)
        wu_raw = keep.tile([P, 8, R], BF16, align_bytes=64)
        wd_view = w_kv_down.rearrange("(m t) k -> m t k", t=4)
        wu_view = w_kv_up.rearrange("(c m) r -> m c r", m=P)
        x_views = [x_bytes[b].rearrange("(s p q) k -> s p q k", p=P, q=4) for b in range(B)]
        x_tiles = {}

        def load_x(pair):
            b, s, h = pair // 4, pair // 2 % 2, pair % 2
            x_codes = work.tile([P, 2, C], U8, tag="x_codes", bufs=PAIRS, align_bytes=64, name="x_codes")
            nc.sync.dma_start(out=x_codes[:], in_=x_views[b][s][:, 2 * h : 2 * h + 2, :])
            x_tiles[pair] = x_codes

        nc.scalar.dma_start(out=gain[:], in_=k_norm_w.partition_broadcast(P))
        load_x(0)
        nc.sync.dma_start(out=scale[:], in_=x_scale[0, 0].rearrange("(g p t) -> p g t", p=P, t=4))
        nc.sync.dma_start(out=wd_raw[:, 0:2, :], in_=wd_view[:, 0:2, :])
        nc.sync.dma_start(out=cos_sb[:], in_=freqs_cos.rearrange("(s p q) j -> p s q j", p=P, q=4))
        nc.sync.dma_start(out=sin_sb[:], in_=freqs_sin.rearrange("(s p q) j -> p s q j", p=P, q=4))
        load_x(1)
        nc.sync.dma_start(out=wd_raw[:, 2:4, :], in_=wd_view[:, 2:4, :])
        nc.sync.dma_start(out=scale_row[:], in_=x_scale[0, 0].partition_broadcast(P))
        load_x(2)
        nc.sync.dma_start(out=wu_raw[:, 0:4, :], in_=wu_view[:, 0:4, :])
        nc.sync.dma_start(out=wu_raw[:, 4:8, :], in_=wu_view[:, 4:8, :])
        for pair in range(3, PAIRS):
            load_x(pair)

        half = D // 2
        gain_pairs = gain[:].rearrange("p (j e) -> p j e", e=2)
        gain_crossed = keep.tile([P, 2, half], F32)
        nc.gpsimd.tensor_scalar(out=gain_crossed[:, 0], in0=gain_pairs[:, :, 1], scalar1=-1.0, scalar2=None, op0=ALU.mult)
        nc.gpsimd.tensor_copy(out=gain_crossed[:, 1], in_=gain_pairs[:, :, 0])
        table_a = keep.tile([P, 8, half, 2], F32)
        table_b = keep.tile([P, 8, 2, half], F32)
        nc.gpsimd.tensor_tensor(
            out=table_a[:],
            in0=cos_sb[:].rearrange("p s q j -> p (s q) j").unsqueeze(3).broadcast_to([P, 8, half, 2]),
            in1=gain_pairs.unsqueeze(1).broadcast_to([P, 8, half, 2]),
            op=ALU.mult,
        )
        nc.gpsimd.tensor_tensor(
            out=table_b[:],
            in0=sin_sb[:].rearrange("p s q j -> p (s q) j").unsqueeze(2).broadcast_to([P, 8, 2, half]),
            in1=gain_crossed[:].unsqueeze(1).broadcast_to([P, 8, 2, half]),
            op=ALU.mult,
        )

        wd_grouped = keep.tile([P, 2, 2, 256, 4], BF16, align_bytes=64)
        wu_grouped = keep.tile([P, 2, 512, 4], BF16, align_bytes=64)
        wd_codes = keep.tile([P, 2, 2, 256], U32, align_bytes=64)
        wd_scales = keep.tile([P, 2, 2, 256], U8, align_bytes=64)
        wu_codes = keep.tile([P, 2, 512], U32, align_bytes=64)
        wu_scales = keep.tile([P, 2, 512], U8, align_bytes=64)

        banks = {}

        def bank_tile(tag, shape):
            bank = psum.tile(shape, F32, tag=tag, bufs=BUFS[tag], name="bank")
            return bank

        def warm_up(count):
            for n in range(count):
                bank = bank_tile("vb", [P, 512])
                nc.tensor.matmul(bank[:], lhsT=warm[:, 0:P], rhs=warm[:], start=True, stop=True)

        def turn_words(out, words, first):
            for u in range(2):
                nc.tensor.transpose(out[:, u], words[:, first + u : first + 256 : 2], ident[:])

        def wd_turn(th, tag):
            for g in range(2):
                bank = bank_tile(tag, [P, 2, 256])
                for i in range(2):
                    turn_words(bank[:, :, SUB * i : SUB * (i + 1)], wd_raw[:, 2 * th + i, :].bitcast(F32), 256 * g)
                banks["wd", th, g] = bank

        def wu_turn(part, tags):
            for i in range(2):
                bank = bank_tile(tags[i], [P, 2, 256])
                for j in range(2):
                    turn_words(bank[:, :, SUB * j : SUB * (j + 1)], wu_raw[:, 4 * part + 2 * i + j, :].bitcast(F32), 0)
                banks["wu", part, i] = bank

        def copy_words(copy, grouped, bank):
            copy(out=grouped.rearrange("p n t -> p (n t)").bitcast(F32).rearrange("p (n u) -> p n u", u=2), in_=bank[:].rearrange("p u n -> p n u"))

        def wd_out(copy, th, g):
            copy_words(copy, wd_grouped[:, th, g], banks["wd", th, g])

        def wu_out(copy, part, i):
            copy_words(copy, wu_grouped[:, part, 256 * i : 256 * (i + 1)], banks["wu", part, i])

        def wd_quant(th):
            nc.vector.quantize_mx(
                out=wd_codes[:, th].rearrange("p g n -> p (g n)").bitcast(FP8X4),
                scales=wd_scales[:, th].rearrange("p g n -> p (g n)"),
                in_=wd_grouped[:, th].rearrange("p g n t -> p (g n t)"),
            )

        def wu_quant(part):
            nc.vector.quantize_mx(out=wu_codes[:, part].bitcast(FP8X4), scales=wu_scales[:, part], in_=wu_grouped[:, part].rearrange("p n t -> p (n t)"))

        wide, xg, xq, xs, lat, lq, ls, rs, products = {}, {}, {}, {}, {}, {}, {}, {}, {}
        kout, vout = {}, {}

        def live(pair):
            return 0 <= pair < PAIRS

        def wide_tile(pair):
            x_wide = work.tile([P, 2, C], BF16, tag="x_wide", bufs=AHEAD + 1, align_bytes=64, name="x_wide")
            wide[pair] = x_wide

        def widen(pair, a, copy):
            if a == 0:
                wide_tile(pair)
            copy(out=wide[pair][:, a, :], in_=x_tiles[pair][:, a, :].bitcast(FP8))

        def premult(pair, a):
            if not EARLY <= pair < PAIRS:
                return
            if a == 0:
                wide_tile(pair)
            nc.vector.tensor_tensor(out=wide[pair][:, a, :], in0=x_tiles[pair][:, a, :].bitcast(FP8), in1=scale_row[:], op=ALU.mult)

        def turn(pair, g):
            if not live(pair):
                return
            bank = bank_tile("xt%d" % g, [P, 2, 256])
            for a in range(2):
                turn_words(bank[:, :, SUB * a : SUB * (a + 1)], wide[pair][:, a, :].bitcast(F32), 256 * g)
            banks["xt", pair, g] = bank

        def x_out(pair, g, copy=nc.scalar.copy):
            if not live(pair):
                return
            if g == 0:
                x_grouped = work.tile([P, 2, 256, 4], BF16, tag="x_grouped", align_bytes=64, name="x_grouped")
                xg[pair] = x_grouped
            bank = banks["xt", pair, g]
            if pair >= EARLY:
                copy_words(copy, xg[pair][:, g], bank)
            else:
                nc.vector.tensor_tensor(
                    out=xg[pair][:, g].rearrange("p n (u e) -> p n u e", u=2),
                    in0=bank[:].rearrange("p u n -> p (u n)").bitcast(BF16).rearrange("p (u n e) -> p n u e", u=2, e=2),
                    in1=scale[:, g, :].rearrange("p (u e) -> p u e", u=2).unsqueeze(1).broadcast_to([P, 256, 2, 2]),
                    op=ALU.mult,
                )

        def quant(pair):
            if not live(pair):
                return
            x_q = work.tile([P, 2, 256], U32, tag="x_q", bufs=AHEAD + 1, align_bytes=64, name="x_q")
            x_s = work.tile([P, 2, 256], U8, tag="x_s", bufs=AHEAD + 1, align_bytes=64, name="x_s")
            nc.vector.quantize_mx(
                out=x_q[:].rearrange("p g n -> p (g n)").bitcast(FP8X4),
                scales=x_s[:].rearrange("p g n -> p (g n)"),
                in_=xg[pair][:].rearrange("p g n t -> p (g n t)"),
            )
            xq[pair], xs[pair] = x_q, x_s

        def down(pair, a):
            if not live(pair):
                return
            bank = bank_tile("lat", [P, 4, SUB])
            cols = slice(SUB * a, SUB * (a + 1))
            for t in range(4):
                th, wcols = t // 2, slice(SUB * (t % 2), SUB * (t % 2 + 1))
                for g in range(2):
                    nc.tensor.matmul_mx(
                        out=bank[:, t, :],
                        lhsT=wd_codes[:, th, g, wcols].bitcast(FP8X4),
                        lhsT_scale=wd_scales[:, th, g, wcols],
                        rhs=xq[pair][:, g, cols].bitcast(FP8X4),
                        rhs_scale=xs[pair][:, g, cols],
                        start=(g == 0),
                        stop=(g == 1),
                    )
            banks["lat", pair, a] = bank

        def latent_out(pair, a, copy=nc.scalar.copy):
            if not live(pair):
                return
            latent = work.tile([P, SUB, 4], BF16, tag="latent", bufs=4, align_bytes=64, name="latent")
            copy(out=latent[:], in_=banks["lat", pair, a][:].rearrange("p t n -> p n t"))
            lat[pair, a] = latent

        def latent_quant(pair, a):
            if not live(pair):
                return
            l_q = work.tile([P, SUB], U32, tag="l_q", bufs=4, align_bytes=64, name="l_q")
            l_s = work.tile([P, SUB], U8, tag="l_s", bufs=4, align_bytes=64, name="l_s")
            nc.vector.quantize_mx(out=l_q[:].bitcast(FP8X4), scales=l_s[:], in_=lat[pair, a][:].rearrange("p n t -> p (n t)"))
            lq[pair, a], ls[pair, a] = l_q, l_s

        def up_pass(bank, pair, a, part):
            nc.tensor.matmul_mx(
                out=bank[:],
                lhsT=lq[pair, a][:].bitcast(FP8X4),
                lhsT_scale=ls[pair, a][:],
                rhs=wu_codes[:, part].bitcast(FP8X4),
                rhs_scale=wu_scales[:, part],
                start=True,
                stop=True,
            )

        def up(pair):
            if not live(pair):
                return
            for part, tag in ((0, "kb"), (1, "vb")):
                for a in range(2):
                    if (tag, pair, a) not in banks:
                        bank = bank_tile(tag, [P, FEAT])
                        banks[tag, pair, a] = bank
                    up_pass(banks[tag, pair, a], pair, a, part)

        def keep_warm(pair, count):
            if not live(pair):
                return
            bank = bank_tile("kb", [P, FEAT])
            for n in range(count):
                nc.tensor.matmul_mx(
                    out=bank[:],
                    lhsT=wd_codes[:, 0, 0, 0:P].bitcast(FP8X4),
                    lhsT_scale=wd_scales[:, 0, 0, 0:P],
                    rhs=wu_codes[:, 0].bitcast(FP8X4),
                    rhs_scale=wu_scales[:, 0],
                    start=True,
                    stop=True,
                )
            banks["kb", pair, 0] = bank

        def norm(pair, a):
            if not live(pair):
                return
            squares = work.tile([P, H], F32, tag="squares", bufs=4, name="squares")
            rstd = work.tile([P, H], F32, tag="rstd", bufs=4, name="rstd")
            for h in range(H):
                junk = work.tile([P, D], BF16, tag="junk", bufs=4, name="junk")
                nc.scalar.activation(out=junk[:], in_=banks["kb", pair, a][:, D * h : D * (h + 1)], func=ACT.Square, accum_out=squares[:, h : h + 1])
            nc.scalar.activation(out=rstd[:], in_=squares[:], func=ACT.Abs_reciprocal_sqrt, bias=EPS, scale=1.0 / D)
            rs[pair, a] = rstd

        def store(out, tile, pair, a):
            b, s, h = pair // 4, pair // 2 % 2, pair % 2
            view = out[b].rearrange("(s p q) h d -> s p q (h d)", p=P, q=4)[s]
            if pair == PAIRS - 1:
                nc.sync.dma_start(out=view[:, 2 * h + a, :], in_=tile[:, a, :])
            elif a == 1:
                nc.sync.dma_start(out=view[:, 2 * h : 2 * h + 2, :], in_=tile[:])

        def values_out(pair, a, copy):
            if not live(pair):
                return
            if a == 0:
                v_tile = work.tile([P, 2, FEAT], F32, tag="v_tile", bufs=4, name="v_tile")
                vout[pair] = v_tile
            copy(out=vout[pair][:, a, :], in_=banks["vb", pair, a][:])
            store(out_1, vout[pair], pair, a)

        def posted(pair, a):
            return a == 0

        def rotate(pair, a, first, last):
            if not live(pair):
                return
            row = (2 * pair + a) % 8
            if first == 0:
                t1 = work.tile([P, H, D], F32, tag="t1", name="t1")
                t2 = work.tile([P, H, 2, half], F32, tag="t2", name="t2")
                products[pair, a] = t1, t2
            t1, t2 = products[pair, a]
            k = banks["kb", pair, a][:].rearrange("p (h d) -> p h d", h=H)
            straight = table_a[:, row].rearrange("p j e -> p (j e)")
            if posted(pair, a):
                if first == 0:
                    nc.vector.tensor_tensor(out=t1[:], in0=k, in1=straight.unsqueeze(1).broadcast_to([P, H, D]), op=ALU.mult)
                if last == 8:
                    nc.vector.tensor_tensor(
                        out=t2[:].rearrange("p h e j -> p e h j"),
                        in0=k.rearrange("p h (j e) -> p e h j", e=2)[:, ::-1],
                        in1=table_b[:, row].unsqueeze(2).broadcast_to([P, 2, H, half]),
                        op=ALU.mult,
                    )
                return
            for n in range(first, last):
                h = n // 2
                if n % 2 == 0:
                    nc.vector.scalar_tensor_tensor(out=t1[:, h], in0=k[:, h], scalar=rs[pair, a][:, h : h + 1], in1=straight, op0=ALU.mult, op1=ALU.mult)
                else:
                    nc.vector.scalar_tensor_tensor(
                        out=t2[:, h], in0=k[:, h].rearrange("p (j e) -> p e j", e=2)[:, ::-1], scalar=rs[pair, a][:, h : h + 1],
                        in1=table_b[:, row], op0=ALU.mult, op1=ALU.mult,
                    )

        def keys_out(pair, a, adder):
            if not live(pair):
                return
            if a == 0:
                k_tile = work.tile([P, 2, FEAT], F32, tag="k_tile", bufs=4, name="k_tile")
                kout[pair] = k_tile
            t1, t2 = products[pair, a]
            adder.tensor_tensor(
                out=kout[pair][:, a, :].rearrange("p (h j e) -> p h j e", h=H, e=2),
                in0=t1[:].rearrange("p h (j e) -> p h j e", e=2),
                in1=t2[:].rearrange("p h e j -> p h j e"),
                op=ALU.add,
            )

        def post(pair, a):
            if not live(pair):
                return
            if not posted(pair, a):
                store(out_0, kout[pair], pair, a)
                return
            for h in range(H):
                head = kout[pair][:, a, D * h : D * (h + 1)]
                nc.scalar.activation(out=head, in_=head, func=ACT.Copy, scale=rs[pair, a][:, h : h + 1])
            store(out_0, kout[pair], pair, a)

        warm_up(WARM)
        widen(0, 0, nc.vector.tensor_copy)
        widen(0, 1, nc.scalar.copy)
        turn(0, 0)
        turn(0, 1)
        warm_up(2)
        widen(1, 0, nc.scalar.copy)
        widen(1, 1, nc.scalar.copy)
        x_out(0, 0)
        x_out(0, 1)
        wd_turn(0, "lat")
        warm_up(2)
        wd_turn(1, "kb")
        warm_up(2)
        turn(1, 0)
        turn(1, 1)
        warm_up(1)
        wd_out(nc.scalar.copy, 0, 0)
        wd_out(nc.vector.tensor_copy, 0, 1)
        wd_out(nc.scalar.copy, 1, 0)
        wd_out(nc.vector.tensor_copy, 1, 1)
        quant(0)
        wd_quant(0)
        wd_quant(1)
        wu_turn(0, ("vb", "vb"))
        down(0, 0)
        down(0, 1)
        wu_out(nc.scalar.copy, 0, 0)
        wu_out(nc.scalar.copy, 0, 1)
        premult(2, 0)
        x_out(1, 0)
        wu_turn(1, ("kb", "kb"))
        latent_out(0, 0)
        latent_out(0, 1)
        premult(2, 1)
        x_out(1, 1)
        wu_quant(0)
        latent_quant(0, 0)
        latent_quant(0, 1)
        wu_out(nc.scalar.copy, 1, 0)
        wu_out(nc.scalar.copy, 1, 1)
        quant(1)
        wu_quant(1)
        for pair in range(3, AHEAD + 1):
            premult(pair, 0)
            premult(pair, 1)

        for s in range(1, PAIRS + 1):
            up(s - 1)
            down(s, 0)
            down(s, 1)
            turn(s + 1, 0)
            turn(s + 1, 1)
            post(s - 2, 0)
            post(s - 2, 1)
            norm(s - 1, 0)
            norm(s - 1, 1)
            premult(s + AHEAD, 0)
            premult(s + AHEAD, 1)
            for a in range(2):
                rotate(s - 1, a, 0, 8)
                keys_out(s - 1, a, nc.vector if s == PAIRS and a == 1 else nc.gpsimd)
            keep_warm(s, 2)
            latent_out(s, 0)
            latent_out(s, 1)
            x_out(s + 1, 0)
            x_out(s + 1, 1)
            values_out(s - 1, 0, nc.scalar.copy)
            values_out(s - 1, 1, nc.scalar.copy)
            latent_quant(s, 0)
            latent_quant(s, 1)
            quant(s + 1)
        post(PAIRS - 1, 0)
        post(PAIRS - 1, 1)
